import numpy as np
import ml_dtypes


def mxq(x, axis, fmt="e4m3"):
    dtype, down = {"e4m3": (ml_dtypes.float8_e4m3fn, 7), "e5m2": (ml_dtypes.float8_e5m2, 14)}[fmt]
    v = np.moveaxis(np.asarray(x, np.float32).astype(ml_dtypes.bfloat16).astype(np.float64), axis, -1)
    blocks = v.reshape(v.shape[:-1] + (-1, 32))
    amax = np.abs(blocks).max(-1, keepdims=True)
    byte = np.maximum(np.where(amax > 0, np.frexp(amax)[1] - 1 + 127, 0) - down, 1)
    scale = np.exp2(byte - 127.0)
    codes = (blocks / scale).astype(np.float32).astype(dtype).astype(np.float64)
    return np.moveaxis((codes * scale).reshape(v.shape), -1, axis)


WIDE = False


def mx_kscale(k):
    if not WIDE:
        return np.ones(k)
    levels = np.array([20, -20, 10, -10, 0])
    a = np.random.permutation(np.resize(levels, k // 512 * 4)).reshape(k // 512, 4)
    idx = np.arange(k)
    return np.exp2(a[idx // 512, idx % 128 // 32])


BF16 = ml_dtypes.bfloat16


def bf(x):
    return np.asarray(x, np.float32).astype(BF16)


def f64(x):
    return np.asarray(x).astype(np.float64)


N, Ci, H, W, Co = 4, 512, 16, 16, 512
TAPS = [(1, 1), (0, 1), (1, 0), (1, 2), (2, 1)]
K = len(TAPS)
PAD = 1


def setup_inputs():
    u = mx_kscale(Co)
    x = np.random.standard_normal((N, Ci, H, W))
    weight = np.random.standard_normal((Co, Ci, K)) / np.sqrt(Ci * K) / u[:, None, None]
    g = np.random.standard_normal((N, Co, H, W)) * np.exp2(np.random.randint(-12, 1, (N, 1, H, W))) * 16.0 * u[None, :, None, None]
    return {"x": bf(x), "weight": bf(weight), "grad_out": bf(g)}


def reference(x, weight, grad_out):
    gq = mxq(f64(grad_out), 1, "e5m2").transpose(1, 0, 2, 3).reshape(Co, N * H * W)
    wq = mxq(f64(weight), 0, "e4m3")
    gx = np.zeros((N, Ci, H, W))
    for k, (dy, dx) in enumerate(TAPS):
        z = (wq[:, :, k].T @ gq).reshape(Ci, N, H, W).transpose(1, 0, 2, 3)
        zp = np.pad(z, ((0, 0), (0, 0), (PAD, PAD), (PAD, PAD)))
        ry, rx = 2 * PAD - dy, 2 * PAD - dx
        gx = gx + zp[:, :, ry:ry + H, rx:rx + W]
    return gx

@@ -1,0 +1,169 @@
+from contextlib import ExitStack
+
+import concourse.mybir as mybir
+
+BF16 = mybir.dt.bfloat16
+F32 = mybir.dt.float32
+I32 = mybir.dt.int32
+U32 = mybir.dt.uint32
+U8 = mybir.dt.uint8
+E4M3X4 = mybir.dt.float8_e4m3fn_x4
+E5M2X4 = mybir.dt.float8_e5m2_x4
+
+P = 128
+PACK = 4
+IMAGES, C_IN, HEIGHT, WIDTH, C_OUT = 4, 512, 16, 16, 512
+TAPS = 5
+AREA = HEIGHT * WIDTH
+ROW = WIDTH * IMAGES
+PIXELS = HEIGHT * ROW
+HALF = PIXELS // 2
+HALF_AREA = AREA // 2
+C_TILES = C_IN // P
+
+TAP_ORDER = (0, 1, 4, 2, 3)
+VECTOR_TAPS = 3
+G_VECTOR_PIXELS = 176
+
+FLOPS = 2 * TAPS * C_OUT * C_IN * IMAGES * AREA
+BYTES = 2 * C_OUT * C_IN * TAPS + 2 * IMAGES * C_OUT * AREA + 4 * IMAGES * C_IN * AREA
+
+
+def tile_spatialconv_pa_kernel(tc, x, weight, grad_out, out):
+    nc = tc.nc
+    with ExitStack() as stack:
+        keep = stack.enter_context(tc.tile_pool(name="keep", bufs=1))
+        pairs = stack.enter_context(tc.tile_pool(name="pairs", bufs=2))
+        chunks = stack.enter_context(tc.tile_pool(name="chunks", bufs=C_TILES))
+        psum = stack.enter_context(tc.psum_pool(name="psum", bufs=2 * C_TILES))
+        stack.enter_context(tc.manual_schedule())
+
+        g_grouped = keep.tile([P, AREA, IMAGES, PACK], BF16, align_bytes=64)
+        g_codes = keep.tile([P, PIXELS + 2 * ROW], U32, align_bytes=64)
+        g_scales = keep.tile([P, PIXELS + 2 * ROW], U8, align_bytes=64)
+        right_codes = keep.tile([P, PIXELS], U32, align_bytes=64)
+        right_scales = keep.tile([P, PIXELS], U8, align_bytes=64)
+        left_codes = keep.tile([P, PIXELS], U32, align_bytes=64)
+        left_scales = keep.tile([P, PIXELS], U8, align_bytes=64)
+        w_codes = keep.tile([P, C_TILES, TAPS, P], U32, align_bytes=64)
+        w_scales = keep.tile([P, C_TILES, TAPS, P], U8, align_bytes=64)
+
+        g_code_rows = g_codes[:].bitcast(I32).rearrange("p (h r) -> p h r", r=ROW)
+        g_scale_rows = g_scales[:].bitcast(I32).rearrange("p (h r) -> p h r", r=WIDTH)
+        right_code_rows = right_codes[:].bitcast(I32).rearrange("p (h r) -> p h r", r=ROW)
+        right_scale_rows = right_scales[:].bitcast(I32).rearrange("p (h r) -> p h r", r=WIDTH)
+        left_code_rows = left_codes[:].bitcast(I32).rearrange("p (h r) -> p h r", r=ROW)
+        left_scale_rows = left_scales[:].bitcast(I32).rearrange("p (h r) -> p h r", r=WIDTH)
+
+        g_raw = []
+        for pair in range(IMAGES // 2):
+            raw = pairs.tile([P, 2, PACK, AREA], BF16, name="g_raw")
+            nc.sync.dma_start(
+                out=raw[:].rearrange("p i j x -> p i (j x)"),
+                in_=grad_out[2 * pair : 2 * pair + 2].rearrange("i (p j) h w -> p i (j h w)", j=PACK),
+            )
+            g_raw.append(raw)
+        w_raw = []
+        for ct in range(C_TILES):
+            raw = chunks.tile([P, PACK, P * TAPS], BF16, name="w_raw")
+            nc.sync.dma_start(
+                out=raw[:],
+                in_=weight[:, ct * P : (ct + 1) * P, :].rearrange("(p j) c t -> p j (c t)", j=PACK),
+            )
+            w_raw.append(raw)
+
+        nc.vector.memset(g_scales[:].bitcast(I32), 0)
+        nc.vector.memset(g_code_rows[:, 0, :], 0)
+        nc.vector.memset(g_code_rows[:, HEIGHT + 1, :], 0)
+        nc.vector.memset(right_code_rows[:, :, ROW - IMAGES :], 0)
+        nc.vector.memset(right_scale_rows[:, :, WIDTH - 1 :], 0)
+        nc.vector.memset(left_code_rows[:, :, :IMAGES], 0)
+        nc.vector.memset(left_scale_rows[:, :, :1], 0)
+
+        for pair in range(IMAGES // 2):
+            source = g_raw[pair][:].rearrange("p i j x -> p x i j")
+            target = g_grouped[:, :, 2 * pair : 2 * pair + 2, :]
+            nc.vector.tensor_copy(out=target[:, :G_VECTOR_PIXELS], in_=source[:, :G_VECTOR_PIXELS])
+            nc.scalar.copy(out=target[:, G_VECTOR_PIXELS:], in_=source[:, G_VECTOR_PIXELS:])
+        for half in range(2):
+            columns = slice(ROW + half * HALF, ROW + (half + 1) * HALF)
+            pixels = slice(half * HALF_AREA, (half + 1) * HALF_AREA)
+            nc.vector.quantize_mx(
+                out=g_codes[:, columns].bitcast(E5M2X4),
+                scales=g_scales[:, columns],
+                in_=g_grouped[:, pixels].rearrange("p x n j -> p (x n j)"),
+            )
+
+        def move_by_one_pixel():
+            image_rows = slice(1, HEIGHT + 1)
+            nc.vector.tensor_copy(out=right_code_rows[:, :, : ROW - IMAGES], in_=g_code_rows[:, image_rows, IMAGES:])
+            nc.vector.tensor_copy(out=right_scale_rows[:, :, : WIDTH - 1], in_=g_scale_rows[:, image_rows, 1:])
+            nc.vector.tensor_copy(out=left_code_rows[:, :, IMAGES:], in_=g_code_rows[:, image_rows, : ROW - IMAGES])
+            nc.vector.tensor_copy(out=left_scale_rows[:, :, 1:], in_=g_scale_rows[:, image_rows, : WIDTH - 1])
+
+        moving = {
+            0: (g_codes, g_scales, ROW),
+            1: (g_codes, g_scales, 2 * ROW),
+            4: (g_codes, g_scales, 0),
+            2: (right_codes, right_scales, 0),
+            3: (left_codes, left_scales, 0),
+        }
+
+        def prepare_weights(ct):
+            w_grouped = chunks.tile([P, TAPS, P, PACK], BF16, align_bytes=64, name="w_grouped")
+            by_tap = w_raw[ct][:].rearrange("p j (c t) -> p t c j", t=TAPS)
+            for place in range(TAPS + 1):
+                if place < TAPS:
+                    tap = TAP_ORDER[place]
+                    if place < VECTOR_TAPS:
+                        nc.vector.tensor_copy(out=w_grouped[:, tap], in_=by_tap[:, tap])
+                    else:
+                        nc.scalar.copy(out=w_grouped[:, tap], in_=by_tap[:, tap])
+                if place > 0:
+                    tap = TAP_ORDER[place - 1]
+                    nc.vector.quantize_mx(
+                        out=w_codes[:, ct, tap, :].bitcast(E4M3X4),
+                        scales=w_scales[:, ct, tap, :],
+                        in_=w_grouped[:, tap].rearrange("p c j -> p (c j)"),
+                    )
+
+        def multiply(ct):
+            banks = []
+            for half in range(2):
+                bank = psum.tile([P, HALF], F32, name="bank")
+                banks.append(bank)
+            for place, tap in enumerate(TAP_ORDER):
+                codes, scales, first = moving[tap]
+                for half in range(2):
+                    columns = slice(first + half * HALF, first + (half + 1) * HALF)
+                    nc.tensor.matmul_mx(
+                        out=banks[half][:],
+                        lhsT=w_codes[:, ct, tap, :].bitcast(E4M3X4),
+                        lhsT_scale=w_scales[:, ct, tap, :],
+                        rhs=codes[:, columns].bitcast(E5M2X4),
+                        rhs_scale=scales[:, columns],
+                        start=(place == 0),
+                        stop=(place == TAPS - 1),
+                    )
+            return banks
+
+        def empty_and_store(ct, banks):
+            result = chunks.tile([P, IMAGES, AREA], F32, name="result")
+            target = out[:, ct * P : (ct + 1) * P].rearrange("n c h w -> c n (h w)")
+            for half in range(2):
+                pixels = slice(half * HALF_AREA, (half + 1) * HALF_AREA)
+                by_image = banks[half][:].rearrange("p (x n) -> p n x", n=IMAGES)
+                if half == 0:
+                    nc.scalar.copy(out=result[:, :, pixels], in_=by_image)
+                else:
+                    nc.vector.tensor_copy(out=result[:, :, pixels], in_=by_image)
+                nc.sync.dma_start(out=target[:, :, pixels], in_=result[:, :, pixels])
+
+        prepare_weights(0)
+        move_by_one_pixel()
+        prepare_weights(1)
+        for ct in range(C_TILES):
+            banks = multiply(ct)
+            if ct + 2 < C_TILES:
+                prepare_weights(ct + 2)
+            empty_and_store(ct, banks)

@@ -111,21 +111,16 @@ def tile_spatialconv_pa_kernel(tc, x, weight, grad_out, out):
 
         def prepare_weights(ct):
             w_grouped = chunks.tile([P, TAPS, P, PACK], BF16, align_bytes=64, name="w_grouped")
-            by_tap = w_raw[ct][:].rearrange("p j (c t) -> p t c j", t=TAPS)
-            for place in range(TAPS + 1):
-                if place < TAPS:
-                    tap = TAP_ORDER[place]
-                    if place < VECTOR_TAPS:
-                        nc.vector.tensor_copy(out=w_grouped[:, tap], in_=by_tap[:, tap])
-                    else:
-                        nc.scalar.copy(out=w_grouped[:, tap], in_=by_tap[:, tap])
-                if place > 0:
-                    tap = TAP_ORDER[place - 1]
-                    nc.vector.quantize_mx(
-                        out=w_codes[:, ct, tap, :].bitcast(E4M3X4),
-                        scales=w_scales[:, ct, tap, :],
-                        in_=w_grouped[:, tap].rearrange("p c j -> p (c j)"),
-                    )
+            source = w_raw[ct][:].rearrange("p j (c t) -> p c j t", t=TAPS)
+            target = w_grouped[:].rearrange("p t c j -> p c j t")
+            nc.vector.tensor_copy(out=target[:, :, :, :VECTOR_TAPS], in_=source[:, :, :, :VECTOR_TAPS])
+            nc.scalar.copy(out=target[:, :, :, VECTOR_TAPS:], in_=source[:, :, :, VECTOR_TAPS:])
+            for tap in range(TAPS):
+                nc.vector.quantize_mx(
+                    out=w_codes[:, ct, tap, :].bitcast(E4M3X4),
+                    scales=w_scales[:, ct, tap, :],
+                    in_=w_grouped[:, tap].rearrange("p c j -> p (c j)"),
+                )
 
         def multiply(ct):
             banks = []

@@ -19,6 +19,7 @@ ROW = WIDTH * IMAGES
 PIXELS = HEIGHT * ROW
 HALF = PIXELS // 2
 HALF_AREA = AREA // 2
+HALF_HEIGHT = HEIGHT // 2
 C_TILES = C_IN // P
 
 TAP_ORDER = (0, 1, 4, 2, 3)
@@ -94,12 +95,13 @@ def tile_spatialconv_pa_kernel(tc, x, weight, grad_out, out):
                 in_=g_grouped[:, pixels].rearrange("p x n j -> p (x n j)"),
             )
 
-        def move_by_one_pixel():
-            image_rows = slice(1, HEIGHT + 1)
-            nc.vector.tensor_copy(out=right_code_rows[:, :, : ROW - IMAGES], in_=g_code_rows[:, image_rows, IMAGES:])
-            nc.vector.tensor_copy(out=right_scale_rows[:, :, : WIDTH - 1], in_=g_scale_rows[:, image_rows, 1:])
-            nc.vector.tensor_copy(out=left_code_rows[:, :, IMAGES:], in_=g_code_rows[:, image_rows, : ROW - IMAGES])
-            nc.vector.tensor_copy(out=left_scale_rows[:, :, 1:], in_=g_scale_rows[:, image_rows, : WIDTH - 1])
+        def move_by_one_pixel(half):
+            rows = slice(half * HALF_HEIGHT, (half + 1) * HALF_HEIGHT)
+            from_rows = slice(1 + half * HALF_HEIGHT, 1 + (half + 1) * HALF_HEIGHT)
+            nc.vector.tensor_copy(out=right_code_rows[:, rows, : ROW - IMAGES], in_=g_code_rows[:, from_rows, IMAGES:])
+            nc.vector.tensor_copy(out=right_scale_rows[:, rows, : WIDTH - 1], in_=g_scale_rows[:, from_rows, 1:])
+            nc.vector.tensor_copy(out=left_code_rows[:, rows, IMAGES:], in_=g_code_rows[:, from_rows, : ROW - IMAGES])
+            nc.vector.tensor_copy(out=left_scale_rows[:, rows, 1:], in_=g_scale_rows[:, from_rows, : WIDTH - 1])
 
         moving = {
             0: (g_codes, g_scales, ROW),
@@ -126,13 +128,11 @@ def tile_spatialconv_pa_kernel(tc, x, weight, grad_out, out):
             banks = []
             for half in range(2):
                 bank = psum.tile([P, HALF], F32, name="bank")
-                banks.append(bank)
-            for place, tap in enumerate(TAP_ORDER):
-                codes, scales, first = moving[tap]
-                for half in range(2):
+                for place, tap in enumerate(TAP_ORDER):
+                    codes, scales, first = moving[tap]
                     columns = slice(first + half * HALF, first + (half + 1) * HALF)
                     nc.tensor.matmul_mx(
-                        out=banks[half][:],
+                        out=bank[:],
                         lhsT=w_codes[:, ct, tap, :].bitcast(E4M3X4),
                         lhsT_scale=w_scales[:, ct, tap, :],
                         rhs=codes[:, columns].bitcast(E5M2X4),
@@ -140,6 +140,7 @@ def tile_spatialconv_pa_kernel(tc, x, weight, grad_out, out):
                         start=(place == 0),
                         stop=(place == TAPS - 1),
                     )
+                banks.append(bank)
             return banks
 
         def empty_and_store(ct, banks):
@@ -155,7 +156,8 @@ def tile_spatialconv_pa_kernel(tc, x, weight, grad_out, out):
                 nc.sync.dma_start(out=target[:, :, pixels], in_=result[:, :, pixels])
 
         prepare_weights(0)
-        move_by_one_pixel()
+        for half in range(2):
+            move_by_one_pixel(half)
         prepare_weights(1)
         for ct in range(C_TILES):
             banks = multiply(ct)

@@ -24,6 +24,7 @@ C_TILES = C_IN // P
 
 TAP_ORDER = (0, 1, 4, 2, 3)
 VECTOR_TAPS = 3
+WARM_PASSES = 3
 G_VECTOR_PIXELS = 176
 
 FLOPS = 2 * TAPS * C_OUT * C_IN * IMAGES * AREA
@@ -72,6 +73,11 @@ def tile_spatialconv_pa_kernel(tc, x, weight, grad_out, out):
                 in_=weight[:, ct * P : (ct + 1) * P, :].rearrange("(p j) c t -> p j (c t)", j=PACK),
             )
             w_raw.append(raw)
+
+        warm_bank = psum.tile([P, HALF], F32, name="bank")
+        for landed in (g_raw[0][:, 0, :2, :].rearrange("p j x -> p (j x)"), g_raw[1][:, 0, :2, :].rearrange("p j x -> p (j x)"), w_raw[0][:, 0, :HALF]):
+            for step in range(WARM_PASSES):
+                nc.tensor.matmul(out=warm_bank[:], lhsT=landed[:, :P], rhs=landed, start=True, stop=True)
 
         nc.vector.memset(g_scales[:].bitcast(I32), 0)
         nc.vector.memset(g_code_rows[:, 0, :], 0)

@@ -22,10 +22,10 @@ HALF_AREA = AREA // 2
 HALF_HEIGHT = HEIGHT // 2
 C_TILES = C_IN // P
 
-TAP_ORDER = (0, 1, 4, 2, 3)
-VECTOR_TAPS = 3
-WARM_PASSES = 3
+WARM_PASSES = (3, 4)
 G_VECTOR_PIXELS = 176
+G_UPPER_SPLIT = 86
+G_LOWER_SPLIT = 50
 
 FLOPS = 2 * TAPS * C_OUT * C_IN * IMAGES * AREA
 BYTES = 2 * C_OUT * C_IN * TAPS + 2 * IMAGES * C_OUT * AREA + 4 * IMAGES * C_IN * AREA
@@ -75,8 +75,9 @@ def tile_spatialconv_pa_kernel(tc, x, weight, grad_out, out):
             w_raw.append(raw)
 
         warm_bank = psum.tile([P, HALF], F32, name="bank")
-        for landed in (g_raw[0][:, 0, :2, :].rearrange("p j x -> p (j x)"), g_raw[1][:, 0, :2, :].rearrange("p j x -> p (j x)"), w_raw[0][:, 0, :HALF]):
-            for step in range(WARM_PASSES):
+        for pair in range(IMAGES // 2):
+            landed = g_raw[pair][:, 0, :2, :].rearrange("p j x -> p (j x)")
+            for step in range(WARM_PASSES[pair]):
                 nc.tensor.matmul(out=warm_bank[:], lhsT=landed[:, :P], rhs=landed, start=True, stop=True)
 
         nc.vector.memset(g_scales[:].bitcast(I32), 0)
@@ -87,11 +88,17 @@ def tile_spatialconv_pa_kernel(tc, x, weight, grad_out, out):
         nc.vector.memset(left_code_rows[:, :, :IMAGES], 0)
         nc.vector.memset(left_scale_rows[:, :, :1], 0)
 
-        for pair in range(IMAGES // 2):
+        def regroup_g(engine_copy, pair, first, last):
             source = g_raw[pair][:].rearrange("p i j x -> p x i j")
             target = g_grouped[:, :, 2 * pair : 2 * pair + 2, :]
-            nc.vector.tensor_copy(out=target[:, :G_VECTOR_PIXELS], in_=source[:, :G_VECTOR_PIXELS])
-            nc.scalar.copy(out=target[:, G_VECTOR_PIXELS:], in_=source[:, G_VECTOR_PIXELS:])
+            engine_copy(out=target[:, first:last], in_=source[:, first:last])
+
+        regroup_g(nc.vector.tensor_copy, 0, 0, G_VECTOR_PIXELS)
+        regroup_g(nc.scalar.copy, 0, G_VECTOR_PIXELS, AREA)
+        regroup_g(nc.vector.tensor_copy, 1, 0, G_UPPER_SPLIT)
+        regroup_g(nc.scalar.copy, 1, G_UPPER_SPLIT, HALF_AREA)
+        regroup_g(nc.vector.tensor_copy, 1, HALF_AREA, HALF_AREA + G_LOWER_SPLIT)
+        regroup_g(nc.scalar.copy, 1, HALF_AREA + G_LOWER_SPLIT, AREA)
         for half in range(2):
             columns = slice(ROW + half * HALF, ROW + (half + 1) * HALF)
             pixels = slice(half * HALF_AREA, (half + 1) * HALF_AREA)
@@ -101,13 +108,13 @@ def tile_spatialconv_pa_kernel(tc, x, weight, grad_out, out):
                 in_=g_grouped[:, pixels].rearrange("p x n j -> p (x n j)"),
             )
 
-        def move_by_one_pixel(half):
-            rows = slice(half * HALF_HEIGHT, (half + 1) * HALF_HEIGHT)
-            from_rows = slice(1 + half * HALF_HEIGHT, 1 + (half + 1) * HALF_HEIGHT)
-            nc.vector.tensor_copy(out=right_code_rows[:, rows, : ROW - IMAGES], in_=g_code_rows[:, from_rows, IMAGES:])
-            nc.vector.tensor_copy(out=right_scale_rows[:, rows, : WIDTH - 1], in_=g_scale_rows[:, from_rows, 1:])
-            nc.vector.tensor_copy(out=left_code_rows[:, rows, IMAGES:], in_=g_code_rows[:, from_rows, : ROW - IMAGES])
-            nc.vector.tensor_copy(out=left_scale_rows[:, rows, 1:], in_=g_scale_rows[:, from_rows, : WIDTH - 1])
+        def move_right():
+            nc.vector.tensor_copy(out=right_code_rows[:, :, : ROW - IMAGES], in_=g_code_rows[:, 1 : HEIGHT + 1, IMAGES:])
+            nc.vector.tensor_copy(out=right_scale_rows[:, :, : WIDTH - 1], in_=g_scale_rows[:, 1 : HEIGHT + 1, 1:])
+
+        def move_left():
+            nc.vector.tensor_copy(out=left_code_rows[:, :, IMAGES:], in_=g_code_rows[:, 1 : HEIGHT + 1, : ROW - IMAGES])
+            nc.vector.tensor_copy(out=left_scale_rows[:, :, 1:], in_=g_scale_rows[:, 1 : HEIGHT + 1, : WIDTH - 1])
 
         moving = {
             0: (g_codes, g_scales, ROW),
@@ -117,56 +124,90 @@ def tile_spatialconv_pa_kernel(tc, x, weight, grad_out, out):
             3: (left_codes, left_scales, 0),
         }
 
-        def prepare_weights(ct):
-            w_grouped = chunks.tile([P, TAPS, P, PACK], BF16, align_bytes=64, name="w_grouped")
-            source = w_raw[ct][:].rearrange("p j (c t) -> p c j t", t=TAPS)
-            target = w_grouped[:].rearrange("p t c j -> p c j t")
-            nc.vector.tensor_copy(out=target[:, :, :, :VECTOR_TAPS], in_=source[:, :, :, :VECTOR_TAPS])
-            nc.scalar.copy(out=target[:, :, :, VECTOR_TAPS:], in_=source[:, :, :, VECTOR_TAPS:])
-            for tap in range(TAPS):
-                nc.vector.quantize_mx(
-                    out=w_codes[:, ct, tap, :].bitcast(E4M3X4),
-                    scales=w_scales[:, ct, tap, :],
-                    in_=w_grouped[:, tap].rearrange("p c j -> p (c j)"),
-                )
-
-        def multiply(ct):
-            banks = []
-            for half in range(2):
-                bank = psum.tile([P, HALF], F32, name="bank")
-                for place, tap in enumerate(TAP_ORDER):
-                    codes, scales, first = moving[tap]
-                    columns = slice(first + half * HALF, first + (half + 1) * HALF)
-                    nc.tensor.matmul_mx(
-                        out=bank[:],
-                        lhsT=w_codes[:, ct, tap, :].bitcast(E4M3X4),
-                        lhsT_scale=w_scales[:, ct, tap, :],
-                        rhs=codes[:, columns].bitcast(E5M2X4),
-                        rhs_scale=scales[:, columns],
-                        start=(place == 0),
-                        stop=(place == TAPS - 1),
-                    )
-                banks.append(bank)
-            return banks
-
-        def empty_and_store(ct, banks):
-            result = chunks.tile([P, IMAGES, AREA], F32, name="result")
-            target = out[:, ct * P : (ct + 1) * P].rearrange("n c h w -> c n (h w)")
-            for half in range(2):
-                pixels = slice(half * HALF_AREA, (half + 1) * HALF_AREA)
-                by_image = banks[half][:].rearrange("p (x n) -> p n x", n=IMAGES)
-                if half == 0:
-                    nc.scalar.copy(out=result[:, :, pixels], in_=by_image)
-                else:
-                    nc.vector.tensor_copy(out=result[:, :, pixels], in_=by_image)
-                nc.sync.dma_start(out=target[:, :, pixels], in_=result[:, :, pixels])
-
-        prepare_weights(0)
-        for half in range(2):
-            move_by_one_pixel(half)
-        prepare_weights(1)
+        w_grouped = []
         for ct in range(C_TILES):
-            banks = multiply(ct)
-            if ct + 2 < C_TILES:
-                prepare_weights(ct + 2)
-            empty_and_store(ct, banks)
+            grouped = chunks.tile([P, TAPS, P, PACK], BF16, align_bytes=64, name="w_grouped")
+            w_grouped.append(grouped)
+
+        def regroup_w(engine_copy, ct, first, last):
+            source = w_raw[ct][:].rearrange("p j (c t) -> p c j t", t=TAPS)
+            target = w_grouped[ct][:].rearrange("p t c j -> p c j t")
+            engine_copy(out=target[:, :, :, first:last], in_=source[:, :, :, first:last])
+
+        def quantise_w(ct, first, last):
+            nc.vector.quantize_mx(
+                out=w_codes[:, ct, first:last, :].rearrange("p t c -> p (t c)").bitcast(E4M3X4),
+                scales=w_scales[:, ct, first:last, :].rearrange("p t c -> p (t c)"),
+                in_=w_grouped[ct][:, first:last].rearrange("p t c j -> p (t c j)"),
+            )
+
+        banks = {}
+
+        def multiply(ct, half, tap, start, stop):
+            if start:
+                bank = psum.tile([P, HALF], F32, name="bank")
+                banks[(ct, half)] = bank
+            codes, scales, first = moving[tap]
+            columns = slice(first + half * HALF, first + (half + 1) * HALF)
+            nc.tensor.matmul_mx(
+                out=banks[(ct, half)][:],
+                lhsT=w_codes[:, ct, tap, :].bitcast(E4M3X4),
+                lhsT_scale=w_scales[:, ct, tap, :],
+                rhs=codes[:, columns].bitcast(E5M2X4),
+                rhs_scale=scales[:, columns],
+                start=start,
+                stop=stop,
+            )
+
+        results = {}
+
+        def empty_and_store(engine_copy, ct, half):
+            if half == 0:
+                result = chunks.tile([P, IMAGES, AREA], F32, name="result")
+                results[ct] = result
+            target = out[:, ct * P : (ct + 1) * P].rearrange("n c h w -> c n (h w)")
+            pixels = slice(half * HALF_AREA, (half + 1) * HALF_AREA)
+            by_image = banks[(ct, half)][:].rearrange("p (x n) -> p n x", n=IMAGES)
+            engine_copy(out=results[ct][:, :, pixels], in_=by_image)
+            nc.sync.dma_start(out=target[:, :, pixels], in_=results[ct][:, :, pixels])
+
+        regroup_w(nc.scalar.copy, 0, 0, 1)
+        regroup_w(nc.scalar.copy, 0, 4, 5)
+        regroup_w(nc.scalar.copy, 1, 0, 2)
+        regroup_w(nc.scalar.copy, 0, 2, 4)
+        regroup_w(nc.scalar.copy, 1, 2, 4)
+        quantise_w(0, 0, 1)
+        regroup_w(nc.vector.tensor_copy, 0, 1, 2)
+        quantise_w(0, 4, 5)
+        quantise_w(0, 1, 2)
+        regroup_w(nc.vector.tensor_copy, 1, 4, 5)
+        quantise_w(1, 0, 2)
+        quantise_w(1, 4, 5)
+        move_right()
+        quantise_w(0, 2, 4)
+        move_left()
+        quantise_w(1, 2, 4)
+        for ct, taps in ((0, (0, 4, 1)), (1, (0, 1, 4))):
+            for place, tap in enumerate(taps):
+                for half in range(2):
+                    multiply(ct, half, tap, place == 0, False)
+        for ct in range(2):
+            for half in range(2):
+                multiply(ct, half, 2, False, False)
+                multiply(ct, half, 3, False, True)
+
+        for ct in range(2, C_TILES):
+            regroup_w(nc.scalar.copy, ct, 2, 4)
+            regroup_w(nc.vector.tensor_copy, ct, 0, 2)
+            regroup_w(nc.vector.tensor_copy, ct, 4, 5)
+            quantise_w(ct, 0, 2)
+            quantise_w(ct, 4, 5)
+            quantise_w(ct, 2, 4)
+            for half in range(2):
+                empty_and_store(nc.scalar.copy, ct - 2, half)
+            for half in range(2):
+                for place, tap in enumerate((0, 1, 4, 2, 3)):
+                    multiply(ct, half, tap, place == 0, place == TAPS - 1)
+        for ct in range(2, C_TILES):
+            empty_and_store(nc.scalar.copy, ct, 0)
+            empty_and_store(nc.vector.tensor_copy, ct, 1)

@@ -23,9 +23,10 @@ HALF_HEIGHT = HEIGHT // 2
 C_TILES = C_IN // P
 
 WARM_PASSES = (3, 4)
+RUN = 4
 G_VECTOR_PIXELS = 176
-G_UPPER_SPLIT = 86
-G_LOWER_SPLIT = 50
+G_UPPER_SPLIT = 88
+G_LOWER_SPLIT = 48
 
 FLOPS = 2 * TAPS * C_OUT * C_IN * IMAGES * AREA
 BYTES = 2 * C_OUT * C_IN * TAPS + 2 * IMAGES * C_OUT * AREA + 4 * IMAGES * C_IN * AREA
@@ -89,9 +90,9 @@ def tile_spatialconv_pa_kernel(tc, x, weight, grad_out, out):
         nc.vector.memset(left_scale_rows[:, :, :1], 0)
 
         def regroup_g(engine_copy, pair, first, last):
-            source = g_raw[pair][:].rearrange("p i j x -> p x i j")
-            target = g_grouped[:, :, 2 * pair : 2 * pair + 2, :]
-            engine_copy(out=target[:, first:last], in_=source[:, first:last])
+            source = g_raw[pair][:, :, :, first:last].rearrange("p i j (b y) -> p b i j y", y=RUN)
+            target = g_grouped[:, first:last, 2 * pair : 2 * pair + 2, :].rearrange("p (b y) i j -> p b i j y", y=RUN)
+            engine_copy(out=target, in_=source)
 
         regroup_g(nc.vector.tensor_copy, 0, 0, G_VECTOR_PIXELS)
         regroup_g(nc.scalar.copy, 0, G_VECTOR_PIXELS, AREA)

@@ -204,8 +204,10 @@ def tile_spatialconv_pa_kernel(tc, x, weight, grad_out, out):
             quantise_w(ct, 0, 2)
             quantise_w(ct, 4, 5)
             quantise_w(ct, 2, 4)
-            for half in range(2):
-                empty_and_store(nc.scalar.copy, ct - 2, half)
+            if ct == 2:
+                for done in range(2):
+                    for half in range(2):
+                        empty_and_store(nc.scalar.copy, done, half)
             for half in range(2):
                 for place, tap in enumerate((0, 1, 4, 2, 3)):
                     multiply(ct, half, tap, place == 0, place == TAPS - 1)

@@ -174,28 +174,28 @@ def tile_spatialconv_pa_kernel(tc, x, weight, grad_out, out):
 
         regroup_w(nc.scalar.copy, 0, 0, 1)
         regroup_w(nc.scalar.copy, 0, 4, 5)
-        regroup_w(nc.scalar.copy, 1, 0, 2)
+        regroup_w(nc.scalar.copy, 1, 4, 5)
         regroup_w(nc.scalar.copy, 0, 2, 4)
         regroup_w(nc.scalar.copy, 1, 2, 4)
         quantise_w(0, 0, 1)
         regroup_w(nc.vector.tensor_copy, 0, 1, 2)
         quantise_w(0, 4, 5)
         quantise_w(0, 1, 2)
-        regroup_w(nc.vector.tensor_copy, 1, 4, 5)
-        quantise_w(1, 0, 2)
+        regroup_w(nc.vector.tensor_copy, 1, 0, 2)
         quantise_w(1, 4, 5)
+        quantise_w(1, 0, 2)
         move_right()
         quantise_w(0, 2, 4)
         move_left()
         quantise_w(1, 2, 4)
-        for ct, taps in ((0, (0, 4, 1)), (1, (0, 1, 4))):
+        for ct, taps in ((0, (0, 4, 1)), (1, (4, 0, 1))):
             for place, tap in enumerate(taps):
                 for half in range(2):
                     multiply(ct, half, tap, place == 0, False)
         for ct in range(2):
-            for half in range(2):
-                multiply(ct, half, 2, False, False)
-                multiply(ct, half, 3, False, True)
+            for tap in (2, 3):
+                for half in range(2):
+                    multiply(ct, half, tap, False, tap == 3)
 
         for ct in range(2, C_TILES):
             regroup_w(nc.scalar.copy, ct, 2, 4)

@@ -211,6 +211,12 @@ def tile_spatialconv_pa_kernel(tc, x, weight, grad_out, out):
             for half in range(2):
                 for place, tap in enumerate((0, 1, 4, 2, 3)):
                     multiply(ct, half, tap, place == 0, place == TAPS - 1)
-        for ct in range(2, C_TILES):
-            empty_and_store(nc.scalar.copy, ct, 0)
-            empty_and_store(nc.vector.tensor_copy, ct, 1)
+        empty_and_store(nc.scalar.copy, 2, 0)
+        empty_and_store(nc.vector.tensor_copy, 2, 1)
+        empty_and_store(nc.scalar.copy, 3, 0)
+        last = C_TILES - 1
+        target = out[:, last * P : (last + 1) * P].rearrange("n c h w -> c n (h w)")
+        by_image = banks[(last, 1)][:].rearrange("p (x n) -> p n x", n=IMAGES)
+        for first in range(0, IMAGES, 2):
+            nc.vector.tensor_copy(out=results[last][:, first : first + 2, HALF_AREA:], in_=by_image[:, first : first + 2])
+            nc.sync.dma_start(out=target[:, first : first + 2, HALF_AREA:], in_=results[last][:, first : first + 2, HALF_AREA:])

@@ -24,6 +24,7 @@ C_TILES = C_IN // P
 
 WARM_PASSES = (3, 4)
 RUN = 4
+W_RUN = 4
 G_VECTOR_PIXELS = 176
 G_UPPER_SPLIT = 88
 G_LOWER_SPLIT = 48
@@ -131,9 +132,9 @@ def tile_spatialconv_pa_kernel(tc, x, weight, grad_out, out):
             w_grouped.append(grouped)
 
         def regroup_w(engine_copy, ct, first, last):
-            source = w_raw[ct][:].rearrange("p j (c t) -> p c j t", t=TAPS)
-            target = w_grouped[ct][:].rearrange("p t c j -> p c j t")
-            engine_copy(out=target[:, :, :, first:last], in_=source[:, :, :, first:last])
+            source = w_raw[ct][:].rearrange("p j (b y t) -> p b j y t", y=W_RUN, t=TAPS)
+            target = w_grouped[ct][:].rearrange("p t (b y) j -> p b j y t", y=W_RUN)
+            engine_copy(out=target[:, :, :, :, first:last], in_=source[:, :, :, :, first:last])
 
         def quantise_w(ct, first, last):
             nc.vector.quantize_mx(

@@ -43,14 +43,14 @@ def tile_spatialconv_pa_kernel(tc, x, weight, grad_out, out):
         stack.enter_context(tc.manual_schedule())
 
         g_grouped = keep.tile([P, AREA, IMAGES, PACK], BF16, align_bytes=64)
-        g_codes = keep.tile([P, PIXELS + 2 * ROW], U32, align_bytes=64)
-        g_scales = keep.tile([P, PIXELS + 2 * ROW], U8, align_bytes=64)
-        right_codes = keep.tile([P, PIXELS], U32, align_bytes=64)
-        right_scales = keep.tile([P, PIXELS], U8, align_bytes=64)
-        left_codes = keep.tile([P, PIXELS], U32, align_bytes=64)
-        left_scales = keep.tile([P, PIXELS], U8, align_bytes=64)
-        w_codes = keep.tile([P, C_TILES, TAPS, P], U32, align_bytes=64)
-        w_scales = keep.tile([P, C_TILES, TAPS, P], U8, align_bytes=64)
+        g_codes = keep.tile([P, PIXELS + 2 * ROW], U32, align_bytes=256)
+        g_scales = keep.tile([P, PIXELS + 2 * ROW], U8, align_bytes=256)
+        right_codes = keep.tile([P, PIXELS], U32, align_bytes=256)
+        right_scales = keep.tile([P, PIXELS], U8, align_bytes=256)
+        left_codes = keep.tile([P, PIXELS], U32, align_bytes=256)
+        left_scales = keep.tile([P, PIXELS], U8, align_bytes=256)
+        w_codes = keep.tile([P, C_TILES, TAPS, P], U32, align_bytes=256)
+        w_scales = keep.tile([P, C_TILES, TAPS, P], U8, align_bytes=256)
 
         g_code_rows = g_codes[:].bitcast(I32).rearrange("p (h r) -> p h r", r=ROW)
         g_scale_rows = g_scales[:].bitcast(I32).rearrange("p (h r) -> p h r", r=WIDTH)

from contextlib import ExitStack

import concourse.mybir as mybir

BF16 = mybir.dt.bfloat16
F32 = mybir.dt.float32
I32 = mybir.dt.int32
U32 = mybir.dt.uint32
U8 = mybir.dt.uint8
E4M3X4 = mybir.dt.float8_e4m3fn_x4
E5M2X4 = mybir.dt.float8_e5m2_x4

P = 128
PACK = 4
IMAGES, C_IN, HEIGHT, WIDTH, C_OUT = 4, 512, 16, 16, 512
TAPS = 5
AREA = HEIGHT * WIDTH
ROW = WIDTH * IMAGES
PIXELS = HEIGHT * ROW
HALF = PIXELS // 2
HALF_AREA = AREA // 2
HALF_HEIGHT = HEIGHT // 2
C_TILES = C_IN // P

WARM_PASSES = (3, 4)
RUN = 4
W_RUN = 4
G_VECTOR_PIXELS = 176
G_UPPER_SPLIT = 88
G_LOWER_SPLIT = 48

FLOPS = 2 * TAPS * C_OUT * C_IN * IMAGES * AREA
BYTES = 2 * C_OUT * C_IN * TAPS + 2 * IMAGES * C_OUT * AREA + 4 * IMAGES * C_IN * AREA


def tile_spatialconv_pa_kernel(tc, x, weight, grad_out, out):
    nc = tc.nc
    with ExitStack() as stack:
        keep = stack.enter_context(tc.tile_pool(name="keep", bufs=1))
        pairs = stack.enter_context(tc.tile_pool(name="pairs", bufs=2))
        chunks = stack.enter_context(tc.tile_pool(name="chunks", bufs=C_TILES))
        psum = stack.enter_context(tc.psum_pool(name="psum", bufs=2 * C_TILES))
        stack.enter_context(tc.manual_schedule())

        g_grouped = keep.tile([P, AREA, IMAGES, PACK], BF16, align_bytes=64)
        g_codes = keep.tile([P, PIXELS + 2 * ROW], U32, align_bytes=256)
        g_scales = keep.tile([P, PIXELS + 2 * ROW], U8, align_bytes=256)
        right_codes = keep.tile([P, PIXELS], U32, align_bytes=256)
        right_scales = keep.tile([P, PIXELS], U8, align_bytes=256)
        left_codes = keep.tile([P, PIXELS], U32, align_bytes=256)
        left_scales = keep.tile([P, PIXELS], U8, align_bytes=256)
        w_codes = keep.tile([P, C_TILES, TAPS, P], U32, align_bytes=256)
        w_scales = keep.tile([P, C_TILES, TAPS, P], U8, align_bytes=256)

        g_code_rows = g_codes[:].bitcast(I32).rearrange("p (h r) -> p h r", r=ROW)
        g_scale_rows = g_scales[:].bitcast(I32).rearrange("p (h r) -> p h r", r=WIDTH)
        right_code_rows = right_codes[:].bitcast(I32).rearrange("p (h r) -> p h r", r=ROW)
        right_scale_rows = right_scales[:].bitcast(I32).rearrange("p (h r) -> p h r", r=WIDTH)
        left_code_rows = left_codes[:].bitcast(I32).rearrange("p (h r) -> p h r", r=ROW)
        left_scale_rows = left_scales[:].bitcast(I32).rearrange("p (h r) -> p h r", r=WIDTH)

        g_raw = []
        for pair in range(IMAGES // 2):
            raw = pairs.tile([P, 2, PACK, AREA], BF16, name="g_raw")
            nc.sync.dma_start(
                out=raw[:].rearrange("p i j x -> p i (j x)"),
                in_=grad_out[2 * pair : 2 * pair + 2].rearrange("i (p j) h w -> p i (j h w)", j=PACK),
            )
            g_raw.append(raw)
        w_raw = []
        for ct in range(C_TILES):
            raw = chunks.tile([P, PACK, P * TAPS], BF16, name="w_raw")
            nc.sync.dma_start(
                out=raw[:],
                in_=weight[:, ct * P : (ct + 1) * P, :].rearrange("(p j) c t -> p j (c t)", j=PACK),
            )
            w_raw.append(raw)

        warm_bank = psum.tile([P, HALF], F32, name="bank")
        for pair in range(IMAGES // 2):
            landed = g_raw[pair][:, 0, :2, :].rearrange("p j x -> p (j x)")
            for step in range(WARM_PASSES[pair]):
                nc.tensor.matmul(out=warm_bank[:], lhsT=landed[:, :P], rhs=landed, start=True, stop=True)

        nc.vector.memset(g_scales[:].bitcast(I32), 0)
        nc.vector.memset(g_code_rows[:, 0, :], 0)
        nc.vector.memset(g_code_rows[:, HEIGHT + 1, :], 0)
        nc.vector.memset(right_code_rows[:, :, ROW - IMAGES :], 0)
        nc.vector.memset(right_scale_rows[:, :, WIDTH - 1 :], 0)
        nc.vector.memset(left_code_rows[:, :, :IMAGES], 0)
        nc.vector.memset(left_scale_rows[:, :, :1], 0)

        def regroup_g(engine_copy, pair, first, last):
            source = g_raw[pair][:, :, :, first:last].rearrange("p i j (b y) -> p b i j y", y=RUN)
            target = g_grouped[:, first:last, 2 * pair : 2 * pair + 2, :].rearrange("p (b y) i j -> p b i j y", y=RUN)
            engine_copy(out=target, in_=source)

        regroup_g(nc.vector.tensor_copy, 0, 0, G_VECTOR_PIXELS)
        regroup_g(nc.scalar.copy, 0, G_VECTOR_PIXELS, AREA)
        regroup_g(nc.vector.tensor_copy, 1, 0, G_UPPER_SPLIT)
        regroup_g(nc.scalar.copy, 1, G_UPPER_SPLIT, HALF_AREA)
        regroup_g(nc.vector.tensor_copy, 1, HALF_AREA, HALF_AREA + G_LOWER_SPLIT)
        regroup_g(nc.scalar.copy, 1, HALF_AREA + G_LOWER_SPLIT, AREA)
        for half in range(2):
            columns = slice(ROW + half * HALF, ROW + (half + 1) * HALF)
            pixels = slice(half * HALF_AREA, (half + 1) * HALF_AREA)
            nc.vector.quantize_mx(
                out=g_codes[:, columns].bitcast(E5M2X4),
                scales=g_scales[:, columns],
                in_=g_grouped[:, pixels].rearrange("p x n j -> p (x n j)"),
            )

        def move_right():
            nc.vector.tensor_copy(out=right_code_rows[:, :, : ROW - IMAGES], in_=g_code_rows[:, 1 : HEIGHT + 1, IMAGES:])
            nc.vector.tensor_copy(out=right_scale_rows[:, :, : WIDTH - 1], in_=g_scale_rows[:, 1 : HEIGHT + 1, 1:])

        def move_left():
            nc.vector.tensor_copy(out=left_code_rows[:, :, IMAGES:], in_=g_code_rows[:, 1 : HEIGHT + 1, : ROW - IMAGES])
            nc.vector.tensor_copy(out=left_scale_rows[:, :, 1:], in_=g_scale_rows[:, 1 : HEIGHT + 1, : WIDTH - 1])

        moving = {
            0: (g_codes, g_scales, ROW),
            1: (g_codes, g_scales, 2 * ROW),
            4: (g_codes, g_scales, 0),
            2: (right_codes, right_scales, 0),
            3: (left_codes, left_scales, 0),
        }

        w_grouped = []
        for ct in range(C_TILES):
            grouped = chunks.tile([P, TAPS, P, PACK], BF16, align_bytes=64, name="w_grouped")
            w_grouped.append(grouped)

        def regroup_w(engine_copy, ct, first, last):
            source = w_raw[ct][:].rearrange("p j (b y t) -> p b j y t", y=W_RUN, t=TAPS)
            target = w_grouped[ct][:].rearrange("p t (b y) j -> p b j y t", y=W_RUN)
            engine_copy(out=target[:, :, :, :, first:last], in_=source[:, :, :, :, first:last])

        def quantise_w(ct, first, last):
            nc.vector.quantize_mx(
                out=w_codes[:, ct, first:last, :].rearrange("p t c -> p (t c)").bitcast(E4M3X4),
                scales=w_scales[:, ct, first:last, :].rearrange("p t c -> p (t c)"),
                in_=w_grouped[ct][:, first:last].rearrange("p t c j -> p (t c j)"),
            )

        banks = {}

        def multiply(ct, half, tap, start, stop):
            if start:
                bank = psum.tile([P, HALF], F32, name="bank")
                banks[(ct, half)] = bank
            codes, scales, first = moving[tap]
            columns = slice(first + half * HALF, first + (half + 1) * HALF)
            nc.tensor.matmul_mx(
                out=banks[(ct, half)][:],
                lhsT=w_codes[:, ct, tap, :].bitcast(E4M3X4),
                lhsT_scale=w_scales[:, ct, tap, :],
                rhs=codes[:, columns].bitcast(E5M2X4),
                rhs_scale=scales[:, columns],
                start=start,
                stop=stop,
            )

        results = {}

        def empty_and_store(engine_copy, ct, half):
            if half == 0:
                result = chunks.tile([P, IMAGES, AREA], F32, name="result")
                results[ct] = result
            target = out[:, ct * P : (ct + 1) * P].rearrange("n c h w -> c n (h w)")
            pixels = slice(half * HALF_AREA, (half + 1) * HALF_AREA)
            by_image = banks[(ct, half)][:].rearrange("p (x n) -> p n x", n=IMAGES)
            engine_copy(out=results[ct][:, :, pixels], in_=by_image)
            nc.sync.dma_start(out=target[:, :, pixels], in_=results[ct][:, :, pixels])

        regroup_w(nc.scalar.copy, 0, 0, 1)
        regroup_w(nc.scalar.copy, 0, 4, 5)
        regroup_w(nc.scalar.copy, 1, 4, 5)
        regroup_w(nc.scalar.copy, 0, 2, 4)
        regroup_w(nc.scalar.copy, 1, 2, 4)
        quantise_w(0, 0, 1)
        regroup_w(nc.vector.tensor_copy, 0, 1, 2)
        quantise_w(0, 4, 5)
        quantise_w(0, 1, 2)
        regroup_w(nc.vector.tensor_copy, 1, 0, 2)
        quantise_w(1, 4, 5)
        quantise_w(1, 0, 2)
        move_right()
        quantise_w(0, 2, 4)
        move_left()
        quantise_w(1, 2, 4)
        for ct, taps in ((0, (0, 4, 1)), (1, (4, 0, 1))):
            for place, tap in enumerate(taps):
                for half in range(2):
                    multiply(ct, half, tap, place == 0, False)
        for ct in range(2):
            for tap in (2, 3):
                for half in range(2):
                    multiply(ct, half, tap, False, tap == 3)

        for ct in range(2, C_TILES):
            regroup_w(nc.scalar.copy, ct, 2, 4)
            regroup_w(nc.vector.tensor_copy, ct, 0, 2)
            regroup_w(nc.vector.tensor_copy, ct, 4, 5)
            quantise_w(ct, 0, 2)
            quantise_w(ct, 4, 5)
            quantise_w(ct, 2, 4)
            if ct == 2:
                for done in range(2):
                    for half in range(2):
                        empty_and_store(nc.scalar.copy, done, half)
            for half in range(2):
                for place, tap in enumerate((0, 1, 4, 2, 3)):
                    multiply(ct, half, tap, place == 0, place == TAPS - 1)
        empty_and_store(nc.scalar.copy, 2, 0)
        empty_and_store(nc.vector.tensor_copy, 2, 1)
        empty_and_store(nc.scalar.copy, 3, 0)
        last = C_TILES - 1
        target = out[:, last * P : (last + 1) * P].rearrange("n c h w -> c n (h w)")
        by_image = banks[(last, 1)][:].rearrange("p (x n) -> p n x", n=IMAGES)
        for first in range(0, IMAGES, 2):
            nc.vector.tensor_copy(out=results[last][:, first : first + 2, HALF_AREA:], in_=by_image[:, first : first + 2])
            nc.sync.dma_start(out=target[:, first : first + 2, HALF_AREA:], in_=results[last][:, first : first + 2, HALF_AREA:])
